import numpy as np
import ml_dtypes


def mxq(x, axis, fmt="e4m3"):
    dtype, down = {"e4m3": (ml_dtypes.float8_e4m3fn, 7), "e5m2": (ml_dtypes.float8_e5m2, 14)}[fmt]
    v = np.moveaxis(np.asarray(x, np.float32).astype(ml_dtypes.bfloat16).astype(np.float64), axis, -1)
    blocks = v.reshape(v.shape[:-1] + (-1, 32))
    amax = np.abs(blocks).max(-1, keepdims=True)
    byte = np.maximum(np.where(amax > 0, np.frexp(amax)[1] - 1 + 127, 0) - down, 1)
    scale = np.exp2(byte - 127.0)
    codes = (blocks / scale).astype(np.float32).astype(dtype).astype(np.float64)
    return np.moveaxis((codes * scale).reshape(v.shape), -1, axis)


WIDE = False


def mx_kscale(k):
    if not WIDE:
        return np.ones(k)
    levels = np.array([10, -10, 5, -5, 0])
    a = np.random.permutation(np.resize(levels, k // 512 * 4)).reshape(k // 512, 4)
    idx = np.arange(k)
    return np.exp2(a[idx // 512, idx % 128 // 32])


BF16 = ml_dtypes.bfloat16


def bf(x):
    return np.asarray(x, np.float32).astype(BF16)


def f64(x):
    return np.asarray(x).astype(np.float64)


E2M1 = np.array([0.0, 0.5, 1.0, 1.5, 2.0, 3.0, 4.0, 6.0, -0.0, -0.5, -1.0, -1.5, -2.0, -3.0, -4.0, -6.0])


def pack_weight(w, fmt):
    k, n = w.shape
    w = f64(bf(w)).reshape(k // 32, 32, n)
    amax = np.abs(w).max(1)
    if fmt == "e4m3":
        byte = np.frexp(amax)[1] - 1 + 127 - 7
    else:
        mant, ex = np.frexp(amax / 6.0)
        byte = np.where(mant > 0.5, ex, ex - 1) + 127
    byte = np.clip(np.where(amax > 0, byte, 1), 1, 254)
    scaled = (w * np.exp2(127.0 - byte)[:, None, :]).reshape(k, n).astype(np.float32)
    by_word = np.ascontiguousarray(scaled.reshape(k // 512, 128, 4, n).transpose(0, 1, 3, 2))
    if fmt == "e4m3":
        words = by_word.astype(ml_dtypes.float8_e4m3fn).view(np.uint8)
    else:
        c = by_word.astype(ml_dtypes.float4_e2m1fn).view(np.uint8) & 0xF
        words = c[..., 0::2] | (c[..., 1::2] << 4)
    return np.ascontiguousarray(words), np.ascontiguousarray(byte.astype(np.uint8).reshape(k // 512, 16, n))


def unpack_weight(words, scales, fmt):
    g, p, n, _ = words.shape
    if fmt == "e4m3":
        vals = np.ascontiguousarray(words).view(ml_dtypes.float8_e4m3fn).astype(np.float64)
    else:
        nib = np.empty((g, p, n, 4), np.uint8)
        nib[..., 0::2] = words & 0xF
        nib[..., 1::2] = words >> 4
        vals = E2M1[nib]
    vals = vals * np.repeat(np.exp2(scales.astype(np.float64) - 127.0), 8, axis=1)[..., None]
    return vals.transpose(0, 1, 3, 2).reshape(g * 512, n)


B, D, H = 128, 2048, 1536
QH = H % 2**9 == 0
FMT = "e4m3"


def sigmoid(v):
    return 1.0 / (1.0 + np.exp(-v))


def xavier(rows, cols):
    limit = np.sqrt(6.0 / (rows + cols))
    return np.random.uniform(-limit, limit, (rows, cols))


def setup_inputs():
    s = mx_kscale(D)
    t = mx_kscale(H) if QH else np.ones(H)
    inp = {"x": bf(np.random.standard_normal((B, D)) * s), "h0": bf(np.random.standard_normal((B, H)) * t), "c0": bf(np.random.standard_normal((B, H)))}
    for n in ("i", "f", "g", "o"):
        inp["W_i" + n + "_words"], inp["W_i" + n + "_scales"] = pack_weight((xavier(H, D) / s).T, FMT)
        inp["b_i" + n] = bf(np.random.standard_normal(H) * 0.1)
        inp["W_h" + n + "_words"], inp["W_h" + n + "_scales"] = pack_weight((xavier(H, H) / t).T, FMT)
        inp["b_h" + n] = bf(np.random.standard_normal(H) * 0.1)
    return inp


def reference(x, h0, c0,
              W_ii_words, W_ii_scales, b_ii, W_hi_words, W_hi_scales, b_hi,
              W_if_words, W_if_scales, b_if, W_hf_words, W_hf_scales, b_hf,
              W_ig_words, W_ig_scales, b_ig, W_hg_words, W_hg_scales, b_hg,
              W_io_words, W_io_scales, b_io, W_ho_words, W_ho_scales, b_ho):
    Wx = np.concatenate([unpack_weight(W_ii_words, W_ii_scales, FMT).T, unpack_weight(W_if_words, W_if_scales, FMT).T, unpack_weight(W_ig_words, W_ig_scales, FMT).T, unpack_weight(W_io_words, W_io_scales, FMT).T], axis=0)
    Wh = np.concatenate([unpack_weight(W_hi_words, W_hi_scales, FMT).T, unpack_weight(W_hf_words, W_hf_scales, FMT).T, unpack_weight(W_hg_words, W_hg_scales, FMT).T, unpack_weight(W_ho_words, W_ho_scales, FMT).T], axis=0)
    b = np.concatenate([f64(b_ii) + f64(b_hi), f64(b_if) + f64(b_hf), f64(b_ig) + f64(b_hg), f64(b_io) + f64(b_ho)])
    gx = mxq(f64(x), 1, "e4m3") @ Wx.T
    if QH:
        gh = mxq(f64(h0), 1, "e4m3") @ Wh.T
    else:
        gh = f64(h0) @ Wh.T
    gates = gx + gh + b
    i_t = sigmoid(gates[:, 0 * H:1 * H])
    f_t = sigmoid(gates[:, 1 * H:2 * H])
    g_t = np.tanh(gates[:, 2 * H:3 * H])
    o_t = sigmoid(gates[:, 3 * H:4 * H])
    c_t = f_t * c0_f(c0) + i_t * g_t
    h_t = o_t * np.tanh(c_t)
    return (h_t, c_t)


def c0_f(c0):
    return f64(c0)

@@ -1,0 +1,200 @@
+from contextlib import ExitStack
+
+import concourse.mybir as mybir
+from concourse.masks import make_identity
+
+F32 = mybir.dt.float32
+BF16 = mybir.dt.bfloat16
+I32 = mybir.dt.int32
+U32 = mybir.dt.uint32
+U8 = mybir.dt.uint8
+FP8X4 = mybir.dt.float8_e4m3fn_x4
+ACT = mybir.ActivationFunctionType
+ALU = mybir.AluOpType
+
+P = 128
+B, D, H = 128, 2048, 1536
+GX = D // 512
+GH = H // 512
+FLOPS = 2 * B * (D + H) * 4 * H
+RING = 16
+COLS = [(0, 512), (512, 512), (1024, 512)]
+O_COLS = [(0, 512), (512, 512), (1024, 256), (1280, 256)]
+
+
+def tile_lstmcell_w_kernel(
+    tc, x, h0, c0,
+    W_ii_words, W_ii_scales, b_ii, W_hi_words, W_hi_scales, b_hi,
+    W_if_words, W_if_scales, b_if, W_hf_words, W_hf_scales, b_hf,
+    W_ig_words, W_ig_scales, b_ig, W_hg_words, W_hg_scales, b_hg,
+    W_io_words, W_io_scales, b_io, W_ho_words, W_ho_scales, b_ho,
+    out_0, out_1,
+):
+    nc = tc.nc
+    gates = [
+        (W_ii_words, W_ii_scales, b_ii, W_hi_words, W_hi_scales, b_hi, ACT.Sigmoid),
+        (W_if_words, W_if_scales, b_if, W_hf_words, W_hf_scales, b_hf, ACT.Sigmoid),
+        (W_ig_words, W_ig_scales, b_ig, W_hg_words, W_hg_scales, b_hg, ACT.Tanh),
+        (W_io_words, W_io_scales, b_io, W_ho_words, W_ho_scales, b_ho, ACT.Sigmoid),
+    ]
+    with ExitStack() as ctx:
+        keep = ctx.enter_context(tc.tile_pool(name="keep", bufs=1))
+        wring = ctx.enter_context(tc.tile_pool(name="wring", bufs=RING))
+        psum = ctx.enter_context(tc.psum_pool(name="psum", bufs=8))
+
+        planes = keep.tile([P, 8, H], U8, name="planes", align_bytes=64)
+        nc.vector.memset(planes[:, 0:2, :].rearrange("p w n -> p (w n)").bitcast(I32), 0)
+        warm = keep.tile([P, 8], F32, name="warm")
+        nc.vector.memset(warm[:], 0.0)
+        nc.vector.memset(planes[:, 2:8, :].rearrange("p w n -> p (w n)").bitcast(I32), 0)
+        zb = keep.tile([P, 4 * H], BF16, name="zb")
+        nc.vector.memset(zb[:].bitcast(I32), 0)
+        ones = keep.tile([P, P], BF16, name="ones")
+        nc.vector.memset(ones[:], 1.0)
+        ident = keep.tile([P, P], F32, name="ident")
+        make_identity(nc, ident[:])
+        warm2 = keep.tile([P, 8], F32, name="warm2")
+        nc.scalar.activation(out=warm2[:], in_=warm[:], func=ACT.Sigmoid)
+
+        x_sb = keep.tile([P, D], BF16, name="x_sb")
+        nc.sync.dma_start(out=x_sb[:], in_=x)
+        h_sb = keep.tile([P, H], BF16, name="h_sb")
+        nc.sync.dma_start(out=h_sb[:], in_=h0)
+        c0_sb = keep.tile([P, H], BF16, name="c0_sb")
+
+        def load_scales(w, scales, groups):
+            for q in range(4):
+                nc.gpsimd.dma_start(
+                    out=planes[32 * q:32 * q + 4 * groups, w, :].bitcast(F32),
+                    in_=scales[:, 4 * q:4 * q + 4, :].bitcast(F32),
+                )
+
+        def load_words(words, g):
+            wt = wring.tile([P, H], U32, name="wt", tag="wt", align_bytes=64)
+            nc.sync.dma_start(
+                out=wt[:].bitcast(I32),
+                in_=words[g].rearrange("p n t -> p (n t)").bitcast(I32),
+            )
+            return wt
+
+        def issue_gate(gi):
+            wi, si, bi, wh, sh, bh, func = gates[gi]
+            load_scales(2 * gi, si, GX)
+            load_scales(2 * gi + 1, sh, GH)
+            nc.gpsimd.dma_start(out=zb[0:1, gi * H:(gi + 1) * H], in_=bi.rearrange("(o n) -> o n", o=1))
+            nc.gpsimd.dma_start(out=zb[1:2, gi * H:(gi + 1) * H], in_=bh.rearrange("(o n) -> o n", o=1))
+            full = []
+            for g in range(GX):
+                full.append((load_words(wi, g), 2 * gi, g, g))
+            last_full = GH if gi < 3 else 1
+            for g in range(last_full):
+                full.append((load_words(wh, g), 2 * gi + 1, g, GX + g))
+            tails = []
+            if gi == 3:
+                for j, (lo, n) in enumerate(O_COLS):
+                    tl = keep.tile([P, 2, n], U32, name="tail%d" % j, align_bytes=64)
+                    nc.sync.dma_start(
+                        out=tl[:].bitcast(I32),
+                        in_=wh[1:3, :, lo:lo + n, :].rearrange("g p n t -> p g (n t)").bitcast(I32),
+                    )
+                    tails.append(tl)
+            return full, tails
+
+        loaded = {0: issue_gate(0)}
+
+        grouped = keep.tile([P, 4 * (GX + GH) * P], BF16, name="grouped", align_bytes=64)
+        xcodes = keep.tile([P, (GX + GH) * P], U32, name="xcodes", align_bytes=64)
+        xsc = keep.tile([P, (GX + GH) * P], U8, name="xsc", align_bytes=64)
+        xw = x_sb[:].bitcast(F32)
+        hw = h_sb[:].bitcast(F32)
+        srcs = [(xw, g) for g in range(GX)] + [(hw, g) for g in range(GH)]
+        for j in range(4):
+            pair = srcs[2 * j:2 * j + 2]
+            s = len(pair)
+            bank = psum.tile([P, 512], F32, name="tb", tag="bank")
+            for a, (src, g) in enumerate(pair):
+                for u in range(2):
+                    nc.tensor.transpose(
+                        out=bank[:, (2 * a + u) * P:(2 * a + u + 1) * P],
+                        in_=src[:, 256 * g + u:256 * (g + 1):2],
+                        identity=ident[:],
+                    )
+            rd = bank[:, 0:256 * s].rearrange("p (s u b) -> p s b u", s=s, u=2)
+            wr = grouped[:, 1024 * j:1024 * j + 512 * s].bitcast(F32).rearrange(
+                "p (s b u) -> p s b u", s=s, u=2)
+            if j % 2 == 0:
+                nc.vector.tensor_copy(out=wr, in_=rd)
+            else:
+                nc.scalar.copy(out=wr, in_=rd)
+        for j in range(4):
+            s = len(srcs[2 * j:2 * j + 2])
+            nc.vector.quantize_mx(
+                out=xcodes[:, 256 * j:256 * j + 128 * s].bitcast(FP8X4),
+                scales=xsc[:, 256 * j:256 * j + 128 * s],
+                in_=grouped[:, 1024 * j:1024 * j + 512 * s],
+            )
+
+        bias_sb = keep.tile([P, 4 * H], F32, name="bias_sb")
+        i_sb = keep.tile([P, H], F32, name="i_sb")
+        f_sb = keep.tile([P, H], F32, name="f_sb")
+        g_sb = keep.tile([P, H], F32, name="g_sb")
+        c_sb = keep.tile([P, H], F32, name="c_sb")
+        tc_sb = keep.tile([P, H], F32, name="tc_sb")
+        o_sb = keep.tile([P, H], F32, name="o_sb")
+        dst = [i_sb, f_sb, g_sb, o_sb]
+
+        def mx_pass(acc, n, xg, rhs, w, g, lo, start, stop):
+            nc.tensor.matmul_mx(
+                out=acc[:, 0:n],
+                lhsT=xcodes[:, P * xg:P * (xg + 1)].bitcast(FP8X4),
+                lhsT_scale=xsc[:, P * xg:P * (xg + 1)],
+                rhs=rhs.bitcast(FP8X4),
+                rhs_scale=planes[4 * g:P, w, lo:lo + n],
+                start=start,
+                stop=stop,
+            )
+
+        def spread_bias(gi):
+            for c in range(3):
+                lo = gi * H + 512 * c
+                bb = psum.tile([P, 512], F32, name="bb", tag="bank")
+                nc.tensor.matmul(out=bb[:], lhsT=ones[:], rhs=zb[:, lo:lo + 512], start=True, stop=True)
+                nc.scalar.copy(out=bias_sb[:, lo:lo + 512], in_=bb[:])
+
+        for gi in range(4):
+            if gi == 0:
+                nc.sync.dma_start(out=c0_sb[:], in_=c0)
+            if gi + 1 < 4:
+                loaded[gi + 1] = issue_gate(gi + 1)
+            full, tails = loaded[gi]
+            func = gates[gi][6]
+            cols = O_COLS if gi == 3 else COLS
+            accs = []
+            for j in range(len(cols)):
+                acc = psum.tile([P, 512], F32, name="acc", tag="bank")
+                accs.append(acc)
+            npass = GX + GH
+            for ki, (wt, w, g, xg) in enumerate(full):
+                for j, (lo, n) in enumerate(cols):
+                    mx_pass(accs[j], n, xg, wt[:, lo:lo + n], w, g, lo, ki == 0, ki == npass - 1)
+                if ki == 3:
+                    spread_bias(gi)
+            for j, (lo, n) in enumerate(cols):
+                if gi == 3:
+                    for a in range(2):
+                        mx_pass(accs[j], n, GX + 1 + a, tails[j][:, a, :], 7, 1 + a, lo, False, a == 1)
+                cs = slice(lo, lo + n)
+                t = dst[gi]
+                nc.vector.tensor_tensor(out=t[:, cs], in0=accs[j][:, 0:n],
+                                        in1=bias_sb[:, gi * H + lo:gi * H + lo + n], op=ALU.add)
+                nc.scalar.activation(out=t[:, cs], in_=t[:, cs], func=func)
+                if gi == 1:
+                    nc.vector.tensor_tensor(out=f_sb[:, cs], in0=f_sb[:, cs], in1=c0_sb[:, cs], op=ALU.mult)
+                if gi == 2:
+                    nc.vector.tensor_tensor(out=g_sb[:, cs], in0=g_sb[:, cs], in1=i_sb[:, cs], op=ALU.mult)
+                    nc.vector.tensor_tensor(out=c_sb[:, cs], in0=g_sb[:, cs], in1=f_sb[:, cs], op=ALU.add)
+                    nc.scalar.activation(out=tc_sb[:, cs], in_=c_sb[:, cs], func=ACT.Tanh)
+                    nc.scalar.dma_start(out=out_1[:, cs], in_=c_sb[:, cs])
+                if gi == 3:
+                    nc.vector.tensor_tensor(out=o_sb[:, cs], in0=o_sb[:, cs], in1=tc_sb[:, cs], op=ALU.mult)
+                    nc.sync.dma_start(out=out_0[:, cs], in_=o_sb[:, cs])

@@ -62,12 +62,20 @@ def tile_lstmcell_w_kernel(
         nc.sync.dma_start(out=h_sb[:], in_=h0)
         c0_sb = keep.tile([P, H], BF16, name="c0_sb")
 
-        def load_scales(w, scales, groups):
-            for q in range(4):
-                nc.gpsimd.dma_start(
-                    out=planes[32 * q:32 * q + 4 * groups, w, :].bitcast(F32),
-                    in_=scales[:, 4 * q:4 * q + 4, :].bitcast(F32),
-                )
+        pending = []
+        for gi in range(4):
+            for w, scales, groups in ((2 * gi, gates[gi][1], GX), (2 * gi + 1, gates[gi][4], GH)):
+                for q in range(4):
+                    pending.append((w, scales, groups, q))
+
+        def load_scales(count):
+            for rep in range(count):
+                if len(pending) > 0:
+                    w, scales, groups, q = pending.pop(0)
+                    nc.sync.dma_start(
+                        out=planes[32 * q:32 * q + 4 * groups, w, :].bitcast(I32),
+                        in_=scales[:, 4 * q:4 * q + 4, :].bitcast(I32),
+                    )
 
         def load_words(words, g):
             wt = wring.tile([P, H], U32, name="wt", tag="wt", align_bytes=64)
@@ -75,12 +83,11 @@ def tile_lstmcell_w_kernel(
                 out=wt[:].bitcast(I32),
                 in_=words[g].rearrange("p n t -> p (n t)").bitcast(I32),
             )
+            load_scales(2)
             return wt
 
         def issue_gate(gi):
             wi, si, bi, wh, sh, bh, func = gates[gi]
-            load_scales(2 * gi, si, GX)
-            load_scales(2 * gi + 1, sh, GH)
             nc.gpsimd.dma_start(out=zb[0:1, gi * H:(gi + 1) * H], in_=bi.rearrange("(o n) -> o n", o=1))
             nc.gpsimd.dma_start(out=zb[1:2, gi * H:(gi + 1) * H], in_=bh.rearrange("(o n) -> o n", o=1))
             full = []

@@ -46,9 +46,9 @@ def tile_lstmcell_w_kernel(
         nc.vector.memset(planes[:, 0:2, :].rearrange("p w n -> p (w n)").bitcast(I32), 0)
         warm = keep.tile([P, 8], F32, name="warm")
         nc.vector.memset(warm[:], 0.0)
-        nc.vector.memset(planes[:, 2:8, :].rearrange("p w n -> p (w n)").bitcast(I32), 0)
         zb = keep.tile([P, 4 * H], BF16, name="zb")
         nc.vector.memset(zb[:].bitcast(I32), 0)
+        nc.vector.memset(planes[:, 2:8, :].rearrange("p w n -> p (w n)").bitcast(I32), 0)
         ones = keep.tile([P, P], BF16, name="ones")
         nc.vector.memset(ones[:], 1.0)
         ident = keep.tile([P, P], F32, name="ident")
@@ -62,20 +62,17 @@ def tile_lstmcell_w_kernel(
         nc.sync.dma_start(out=h_sb[:], in_=h0)
         c0_sb = keep.tile([P, H], BF16, name="c0_sb")
 
+        def load_scales(w, scales, groups):
+            for q in range(4):
+                nc.gpsimd.dma_start(
+                    out=planes[32 * q:32 * q + 4 * groups, w, :].bitcast(F32),
+                    in_=scales[:, 4 * q:4 * q + 4, :].bitcast(F32),
+                )
+
         pending = []
         for gi in range(4):
-            for w, scales, groups in ((2 * gi, gates[gi][1], GX), (2 * gi + 1, gates[gi][4], GH)):
-                for q in range(4):
-                    pending.append((w, scales, groups, q))
-
-        def load_scales(count):
-            for rep in range(count):
-                if len(pending) > 0:
-                    w, scales, groups, q = pending.pop(0)
-                    nc.sync.dma_start(
-                        out=planes[32 * q:32 * q + 4 * groups, w, :].bitcast(I32),
-                        in_=scales[:, 4 * q:4 * q + 4, :].bitcast(I32),
-                    )
+            pending.append((0, gi, gates[gi][2]))
+            pending.append((1, gi, gates[gi][5]))
 
         def load_words(words, g):
             wt = wring.tile([P, H], U32, name="wt", tag="wt", align_bytes=64)
@@ -83,13 +80,15 @@ def tile_lstmcell_w_kernel(
                 out=wt[:].bitcast(I32),
                 in_=words[g].rearrange("p n t -> p (n t)").bitcast(I32),
             )
-            load_scales(2)
+            if len(pending) > 0:
+                row, bg, vec = pending.pop(0)
+                nc.sync.dma_start(out=zb[row:row + 1, bg * H:(bg + 1) * H], in_=vec.rearrange("(o n) -> o n", o=1))
             return wt
 
         def issue_gate(gi):
             wi, si, bi, wh, sh, bh, func = gates[gi]
-            nc.gpsimd.dma_start(out=zb[0:1, gi * H:(gi + 1) * H], in_=bi.rearrange("(o n) -> o n", o=1))
-            nc.gpsimd.dma_start(out=zb[1:2, gi * H:(gi + 1) * H], in_=bh.rearrange("(o n) -> o n", o=1))
+            load_scales(2 * gi, si, GX)
+            load_scales(2 * gi + 1, sh, GH)
             full = []
             for g in range(GX):
                 full.append((load_words(wi, g), 2 * gi, g, g))

@@ -46,9 +46,9 @@ def tile_lstmcell_w_kernel(
         nc.vector.memset(planes[:, 0:2, :].rearrange("p w n -> p (w n)").bitcast(I32), 0)
         warm = keep.tile([P, 8], F32, name="warm")
         nc.vector.memset(warm[:], 0.0)
+        nc.vector.memset(planes[:, 2:8, :].rearrange("p w n -> p (w n)").bitcast(I32), 0)
         zb = keep.tile([P, 4 * H], BF16, name="zb")
         nc.vector.memset(zb[:].bitcast(I32), 0)
-        nc.vector.memset(planes[:, 2:8, :].rearrange("p w n -> p (w n)").bitcast(I32), 0)
         ones = keep.tile([P, P], BF16, name="ones")
         nc.vector.memset(ones[:], 1.0)
         ident = keep.tile([P, P], F32, name="ident")
@@ -64,9 +64,9 @@ def tile_lstmcell_w_kernel(
 
         def load_scales(w, scales, groups):
             for q in range(4):
-                nc.gpsimd.dma_start(
-                    out=planes[32 * q:32 * q + 4 * groups, w, :].bitcast(F32),
-                    in_=scales[:, 4 * q:4 * q + 4, :].bitcast(F32),
+                nc.sync.dma_start(
+                    out=planes[32 * q:32 * q + 4 * groups, w, :].bitcast(I32),
+                    in_=scales[:, 4 * q:4 * q + 4, :].bitcast(I32),
                 )
 
         pending = []
@@ -87,8 +87,6 @@ def tile_lstmcell_w_kernel(
 
         def issue_gate(gi):
             wi, si, bi, wh, sh, bh, func = gates[gi]
-            load_scales(2 * gi, si, GX)
-            load_scales(2 * gi + 1, sh, GH)
             full = []
             for g in range(GX):
                 full.append((load_words(wi, g), 2 * gi, g, g))
@@ -106,6 +104,9 @@ def tile_lstmcell_w_kernel(
                     tails.append(tl)
             return full, tails
 
+        for gi in range(4):
+            load_scales(2 * gi, gates[gi][1], GX)
+            load_scales(2 * gi + 1, gates[gi][4], GH)
         loaded = {0: issue_gate(0)}
 
         grouped = keep.tile([P, 4 * (GX + GH) * P], BF16, name="grouped", align_bytes=64)

@@ -46,9 +46,9 @@ def tile_lstmcell_w_kernel(
         nc.vector.memset(planes[:, 0:2, :].rearrange("p w n -> p (w n)").bitcast(I32), 0)
         warm = keep.tile([P, 8], F32, name="warm")
         nc.vector.memset(warm[:], 0.0)
-        nc.vector.memset(planes[:, 2:8, :].rearrange("p w n -> p (w n)").bitcast(I32), 0)
         zb = keep.tile([P, 4 * H], BF16, name="zb")
         nc.vector.memset(zb[:].bitcast(I32), 0)
+        nc.vector.memset(planes[:, 2:8, :].rearrange("p w n -> p (w n)").bitcast(I32), 0)
         ones = keep.tile([P, P], BF16, name="ones")
         nc.vector.memset(ones[:], 1.0)
         ident = keep.tile([P, P], F32, name="ident")
@@ -64,10 +64,12 @@ def tile_lstmcell_w_kernel(
 
         def load_scales(w, scales, groups):
             for q in range(4):
-                nc.sync.dma_start(
-                    out=planes[32 * q:32 * q + 4 * groups, w, :].bitcast(I32),
-                    in_=scales[:, 4 * q:4 * q + 4, :].bitcast(I32),
+                nc.gpsimd.dma_start(
+                    out=planes[32 * q:32 * q + 4 * groups, w, :].bitcast(F32),
+                    in_=scales[:, 4 * q:4 * q + 4, :].bitcast(F32),
                 )
+
+        early = [0, 1, 2, 3]
 
         pending = []
         for gi in range(4):
@@ -80,6 +82,13 @@ def tile_lstmcell_w_kernel(
                 out=wt[:].bitcast(I32),
                 in_=words[g].rearrange("p n t -> p (n t)").bitcast(I32),
             )
+            for rep in range(2):
+                if len(early) > 0:
+                    q = early.pop(0)
+                    nc.sync.dma_start(
+                        out=planes[32 * q:32 * q + 16, 0, :].bitcast(I32),
+                        in_=W_ii_scales[:, 4 * q:4 * q + 4, :].bitcast(I32),
+                    )
             if len(pending) > 0:
                 row, bg, vec = pending.pop(0)
                 nc.sync.dma_start(out=zb[row:row + 1, bg * H:(bg + 1) * H], in_=vec.rearrange("(o n) -> o n", o=1))
@@ -87,6 +96,9 @@ def tile_lstmcell_w_kernel(
 
         def issue_gate(gi):
             wi, si, bi, wh, sh, bh, func = gates[gi]
+            if gi > 0:
+                load_scales(2 * gi, si, GX)
+            load_scales(2 * gi + 1, sh, GH)
             full = []
             for g in range(GX):
                 full.append((load_words(wi, g), 2 * gi, g, g))
@@ -104,9 +116,6 @@ def tile_lstmcell_w_kernel(
                     tails.append(tl)
             return full, tails
 
-        for gi in range(4):
-            load_scales(2 * gi, gates[gi][1], GX)
-            load_scales(2 * gi + 1, gates[gi][4], GH)
         loaded = {0: issue_gate(0)}
 
         grouped = keep.tile([P, 4 * (GX + GH) * P], BF16, name="grouped", align_bytes=64)

@@ -20,6 +20,7 @@ FLOPS = 2 * B * (D + H) * 4 * H
 RING = 16
 COLS = [(0, 512), (512, 512), (1024, 512)]
 O_COLS = [(0, 512), (512, 512), (1024, 256), (1280, 256)]
+POOL_MULS = 2
 
 
 def tile_lstmcell_w_kernel(
@@ -41,6 +42,7 @@ def tile_lstmcell_w_kernel(
         keep = ctx.enter_context(tc.tile_pool(name="keep", bufs=1))
         wring = ctx.enter_context(tc.tile_pool(name="wring", bufs=RING))
         psum = ctx.enter_context(tc.psum_pool(name="psum", bufs=8))
+        ctx.enter_context(tc.manual_schedule())
 
         planes = keep.tile([P, 8, H], U8, name="planes", align_bytes=64)
         nc.vector.memset(planes[:, 0:2, :].rearrange("p w n -> p (w n)").bitcast(I32), 0)
@@ -69,8 +71,6 @@ def tile_lstmcell_w_kernel(
                     in_=scales[:, 4 * q:4 * q + 4, :].bitcast(F32),
                 )
 
-        early = [0, 1, 2, 3]
-
         pending = []
         for gi in range(4):
             pending.append((0, gi, gates[gi][2]))
@@ -82,13 +82,6 @@ def tile_lstmcell_w_kernel(
                 out=wt[:].bitcast(I32),
                 in_=words[g].rearrange("p n t -> p (n t)").bitcast(I32),
             )
-            for rep in range(2):
-                if len(early) > 0:
-                    q = early.pop(0)
-                    nc.sync.dma_start(
-                        out=planes[32 * q:32 * q + 16, 0, :].bitcast(I32),
-                        in_=W_ii_scales[:, 4 * q:4 * q + 4, :].bitcast(I32),
-                    )
             if len(pending) > 0:
                 row, bg, vec = pending.pop(0)
                 nc.sync.dma_start(out=zb[row:row + 1, bg * H:(bg + 1) * H], in_=vec.rearrange("(o n) -> o n", o=1))
@@ -96,8 +89,7 @@ def tile_lstmcell_w_kernel(
 
         def issue_gate(gi):
             wi, si, bi, wh, sh, bh, func = gates[gi]
-            if gi > 0:
-                load_scales(2 * gi, si, GX)
+            load_scales(2 * gi, si, GX)
             load_scales(2 * gi + 1, sh, GH)
             full = []
             for g in range(GX):
@@ -105,16 +97,7 @@ def tile_lstmcell_w_kernel(
             last_full = GH if gi < 3 else 1
             for g in range(last_full):
                 full.append((load_words(wh, g), 2 * gi + 1, g, GX + g))
-            tails = []
-            if gi == 3:
-                for j, (lo, n) in enumerate(O_COLS):
-                    tl = keep.tile([P, 2, n], U32, name="tail%d" % j, align_bytes=64)
-                    nc.sync.dma_start(
-                        out=tl[:].bitcast(I32),
-                        in_=wh[1:3, :, lo:lo + n, :].rearrange("g p n t -> p g (n t)").bitcast(I32),
-                    )
-                    tails.append(tl)
-            return full, tails
+            return full
 
         loaded = {0: issue_gate(0)}
 
@@ -177,13 +160,36 @@ def tile_lstmcell_w_kernel(
                 nc.tensor.matmul(out=bb[:], lhsT=ones[:], rhs=zb[:, lo:lo + 512], start=True, stop=True)
                 nc.scalar.copy(out=bias_sb[:, lo:lo + 512], in_=bb[:])
 
+        def gate_value(gi, acc, lo, n):
+            t = dst[gi]
+            nc.vector.tensor_tensor(out=t[:, lo:lo + n], in0=acc[:, 0:n],
+                                    in1=bias_sb[:, gi * H + lo:gi * H + lo + n], op=ALU.add)
+            nc.scalar.activation(out=t[:, lo:lo + n], in_=t[:, lo:lo + n], func=gates[gi][6])
+
+        def h_out(j):
+            lo, n = O_COLS[j]
+            cs = slice(lo, lo + n)
+            eng = nc.gpsimd if j < POOL_MULS else nc.vector
+            eng.tensor_tensor(out=o_sb[:, cs], in0=o_sb[:, cs], in1=tc_sb[:, cs], op=ALU.mult)
+            nc.sync.dma_start(out=out_0[:, cs], in_=o_sb[:, cs])
+
+        tails = []
         for gi in range(4):
             if gi == 0:
                 nc.sync.dma_start(out=c0_sb[:], in_=c0)
             if gi + 1 < 4:
                 loaded[gi + 1] = issue_gate(gi + 1)
-            full, tails = loaded[gi]
-            func = gates[gi][6]
+            if gi == 3:
+                for j, (lo, n) in enumerate(O_COLS):
+                    tl = keep.tile([P, 2, n], U32, name="tail%d" % j, align_bytes=64)
+                    nc.sync.dma_start(
+                        out=tl[:].bitcast(I32),
+                        in_=W_ho_words[1:3, :, lo:lo + n, :].rearrange("g p n t -> p g (n t)").bitcast(I32),
+                    )
+                    tails.append(tl)
+                for lo, n in COLS:
+                    nc.sync.dma_start(out=out_1[:, lo:lo + n], in_=c_sb[:, lo:lo + n])
+            full = loaded[gi]
             cols = O_COLS if gi == 3 else COLS
             accs = []
             for j in range(len(cols)):
@@ -195,22 +201,23 @@ def tile_lstmcell_w_kernel(
                     mx_pass(accs[j], n, xg, wt[:, lo:lo + n], w, g, lo, ki == 0, ki == npass - 1)
                 if ki == 3:
                     spread_bias(gi)
-            for j, (lo, n) in enumerate(cols):
-                if gi == 3:
+            if gi < 3:
+                for j, (lo, n) in enumerate(cols):
+                    gate_value(gi, accs[j], lo, n)
+                for lo, n in cols:
+                    cs = slice(lo, lo + n)
+                    if gi == 1:
+                        nc.vector.tensor_tensor(out=f_sb[:, cs], in0=f_sb[:, cs], in1=c0_sb[:, cs], op=ALU.mult)
+                    if gi == 2:
+                        nc.vector.tensor_tensor(out=g_sb[:, cs], in0=g_sb[:, cs], in1=i_sb[:, cs], op=ALU.mult)
+                        nc.vector.tensor_tensor(out=c_sb[:, cs], in0=g_sb[:, cs], in1=f_sb[:, cs], op=ALU.add)
+                        nc.scalar.activation(out=tc_sb[:, cs], in_=c_sb[:, cs], func=ACT.Tanh)
+            else:
+                for j, (lo, n) in enumerate(cols):
                     for a in range(2):
                         mx_pass(accs[j], n, GX + 1 + a, tails[j][:, a, :], 7, 1 + a, lo, False, a == 1)
-                cs = slice(lo, lo + n)
-                t = dst[gi]
-                nc.vector.tensor_tensor(out=t[:, cs], in0=accs[j][:, 0:n],
-                                        in1=bias_sb[:, gi * H + lo:gi * H + lo + n], op=ALU.add)
-                nc.scalar.activation(out=t[:, cs], in_=t[:, cs], func=func)
-                if gi == 1:
-                    nc.vector.tensor_tensor(out=f_sb[:, cs], in0=f_sb[:, cs], in1=c0_sb[:, cs], op=ALU.mult)
-                if gi == 2:
-                    nc.vector.tensor_tensor(out=g_sb[:, cs], in0=g_sb[:, cs], in1=i_sb[:, cs], op=ALU.mult)
-                    nc.vector.tensor_tensor(out=c_sb[:, cs], in0=g_sb[:, cs], in1=f_sb[:, cs], op=ALU.add)
-                    nc.scalar.activation(out=tc_sb[:, cs], in_=c_sb[:, cs], func=ACT.Tanh)
-                    nc.scalar.dma_start(out=out_1[:, cs], in_=c_sb[:, cs])
-                if gi == 3:
-                    nc.vector.tensor_tensor(out=o_sb[:, cs], in0=o_sb[:, cs], in1=tc_sb[:, cs], op=ALU.mult)
-                    nc.sync.dma_start(out=out_0[:, cs], in_=o_sb[:, cs])
+                    gate_value(gi, accs[j], lo, n)
+                    if j < POOL_MULS:
+                        h_out(j)
+                for j in range(POOL_MULS, len(cols)):
+                    h_out(j)

@@ -20,7 +20,12 @@ FLOPS = 2 * B * (D + H) * 4 * H
 RING = 16
 COLS = [(0, 512), (512, 512), (1024, 512)]
 O_COLS = [(0, 512), (512, 512), (1024, 256), (1280, 256)]
-POOL_MULS = 2
+S_MODE = "mixed"
+PIN = False
+CT_LATE = False
+ADDS_FIRST = False
+POOL_MULS = 0
+BIAS_ON_POOL = True
 
 
 def tile_lstmcell_w_kernel(
@@ -42,7 +47,8 @@ def tile_lstmcell_w_kernel(
         keep = ctx.enter_context(tc.tile_pool(name="keep", bufs=1))
         wring = ctx.enter_context(tc.tile_pool(name="wring", bufs=RING))
         psum = ctx.enter_context(tc.psum_pool(name="psum", bufs=8))
-        ctx.enter_context(tc.manual_schedule())
+        if PIN:
+            ctx.enter_context(tc.manual_schedule())
 
         planes = keep.tile([P, 8, H], U8, name="planes", align_bytes=64)
         nc.vector.memset(planes[:, 0:2, :].rearrange("p w n -> p (w n)").bitcast(I32), 0)
@@ -64,17 +70,32 @@ def tile_lstmcell_w_kernel(
         nc.sync.dma_start(out=h_sb[:], in_=h0)
         c0_sb = keep.tile([P, H], BF16, name="c0_sb")
 
-        def load_scales(w, scales, groups):
-            for q in range(4):
+        def scale_dma(on_sync, w, scales, groups, q):
+            if on_sync:
+                nc.sync.dma_start(
+                    out=planes[32 * q:32 * q + 4 * groups, w, :].bitcast(I32),
+                    in_=scales[:, 4 * q:4 * q + 4, :].bitcast(I32),
+                )
+            else:
                 nc.gpsimd.dma_start(
                     out=planes[32 * q:32 * q + 4 * groups, w, :].bitcast(F32),
                     in_=scales[:, 4 * q:4 * q + 4, :].bitcast(F32),
                 )
 
-        pending = []
+        woven = []
         for gi in range(4):
-            pending.append((0, gi, gates[gi][2]))
-            pending.append((1, gi, gates[gi][5]))
+            for w, scales, groups in ((2 * gi, gates[gi][1], GX), (2 * gi + 1, gates[gi][4], GH)):
+                for q in range(4):
+                    if S_MODE == "sync" or (S_MODE == "mixed" and q < 2):
+                        woven.append((w, scales, groups, q))
+        biases = []
+        for gi in range(4):
+            biases.append((0, gi, gates[gi][2]))
+            biases.append((1, gi, gates[gi][5]))
+        nloads = [0]
+
+        def bias_dma(eng, row, bg, vec):
+            eng.dma_start(out=zb[row:row + 1, bg * H:(bg + 1) * H], in_=vec.rearrange("(o n) -> o n", o=1))
 
         def load_words(words, g):
             wt = wring.tile([P, H], U32, name="wt", tag="wt", align_bytes=64)
@@ -82,15 +103,26 @@ def tile_lstmcell_w_kernel(
                 out=wt[:].bitcast(I32),
                 in_=words[g].rearrange("p n t -> p (n t)").bitcast(I32),
             )
-            if len(pending) > 0:
-                row, bg, vec = pending.pop(0)
-                nc.sync.dma_start(out=zb[row:row + 1, bg * H:(bg + 1) * H], in_=vec.rearrange("(o n) -> o n", o=1))
+            nloads[0] = nloads[0] + 1
+            count = 2 if (S_MODE == "sync" or nloads[0] <= 2) else 1
+            for rep in range(count):
+                if len(woven) > 0:
+                    w, scales, groups, q = woven.pop(0)
+                    scale_dma(True, w, scales, groups, q)
+            if len(biases) > 0 and not BIAS_ON_POOL:
+                row, bg, vec = biases.pop(0)
+                bias_dma(nc.sync, row, bg, vec)
             return wt
 
         def issue_gate(gi):
             wi, si, bi, wh, sh, bh, func = gates[gi]
-            load_scales(2 * gi, si, GX)
-            load_scales(2 * gi + 1, sh, GH)
+            for w, scales, groups in ((2 * gi, si, GX), (2 * gi + 1, sh, GH)):
+                for q in range(4):
+                    if S_MODE == "pool" or (S_MODE == "mixed" and q >= 2):
+                        scale_dma(False, w, scales, groups, q)
+            if BIAS_ON_POOL:
+                bias_dma(nc.gpsimd, 0, gi, bi)
+                bias_dma(nc.gpsimd, 1, gi, bh)
             full = []
             for g in range(GX):
                 full.append((load_words(wi, g), 2 * gi, g, g))
@@ -98,6 +130,17 @@ def tile_lstmcell_w_kernel(
             for g in range(last_full):
                 full.append((load_words(wh, g), 2 * gi + 1, g, GX + g))
             return full
+
+        tails = []
+
+        def issue_tails():
+            for j, (lo, n) in enumerate(O_COLS):
+                tl = keep.tile([P, 2, n], U32, name="tail%d" % j, align_bytes=64)
+                nc.sync.dma_start(
+                    out=tl[:].bitcast(I32),
+                    in_=W_ho_words[1:3, :, lo:lo + n, :].rearrange("g p n t -> p g (n t)").bitcast(I32),
+                )
+                tails.append(tl)
 
         loaded = {0: issue_gate(0)}
 
@@ -166,6 +209,17 @@ def tile_lstmcell_w_kernel(
                                     in1=bias_sb[:, gi * H + lo:gi * H + lo + n], op=ALU.add)
             nc.scalar.activation(out=t[:, lo:lo + n], in_=t[:, lo:lo + n], func=gates[gi][6])
 
+        def after(gi, lo, n):
+            cs = slice(lo, lo + n)
+            if gi == 1:
+                nc.vector.tensor_tensor(out=f_sb[:, cs], in0=f_sb[:, cs], in1=c0_sb[:, cs], op=ALU.mult)
+            if gi == 2:
+                nc.vector.tensor_tensor(out=g_sb[:, cs], in0=g_sb[:, cs], in1=i_sb[:, cs], op=ALU.mult)
+                nc.vector.tensor_tensor(out=c_sb[:, cs], in0=g_sb[:, cs], in1=f_sb[:, cs], op=ALU.add)
+                nc.scalar.activation(out=tc_sb[:, cs], in_=c_sb[:, cs], func=ACT.Tanh)
+                if not CT_LATE:
+                    nc.scalar.dma_start(out=out_1[:, cs], in_=c_sb[:, cs])
+
         def h_out(j):
             lo, n = O_COLS[j]
             cs = slice(lo, lo + n)
@@ -173,20 +227,15 @@ def tile_lstmcell_w_kernel(
             eng.tensor_tensor(out=o_sb[:, cs], in0=o_sb[:, cs], in1=tc_sb[:, cs], op=ALU.mult)
             nc.sync.dma_start(out=out_0[:, cs], in_=o_sb[:, cs])
 
-        tails = []
         for gi in range(4):
             if gi == 0:
                 nc.sync.dma_start(out=c0_sb[:], in_=c0)
             if gi + 1 < 4:
                 loaded[gi + 1] = issue_gate(gi + 1)
-            if gi == 3:
-                for j, (lo, n) in enumerate(O_COLS):
-                    tl = keep.tile([P, 2, n], U32, name="tail%d" % j, align_bytes=64)
-                    nc.sync.dma_start(
-                        out=tl[:].bitcast(I32),
-                        in_=W_ho_words[1:3, :, lo:lo + n, :].rearrange("g p n t -> p g (n t)").bitcast(I32),
-                    )
-                    tails.append(tl)
+                if gi + 1 == 3 and not CT_LATE:
+                    issue_tails()
+            if gi == 3 and CT_LATE:
+                issue_tails()
                 for lo, n in COLS:
                     nc.sync.dma_start(out=out_1[:, lo:lo + n], in_=c_sb[:, lo:lo + n])
             full = loaded[gi]
@@ -202,22 +251,24 @@ def tile_lstmcell_w_kernel(
                 if ki == 3:
                     spread_bias(gi)
             if gi < 3:
-                for j, (lo, n) in enumerate(cols):
-                    gate_value(gi, accs[j], lo, n)
-                for lo, n in cols:
-                    cs = slice(lo, lo + n)
-                    if gi == 1:
-                        nc.vector.tensor_tensor(out=f_sb[:, cs], in0=f_sb[:, cs], in1=c0_sb[:, cs], op=ALU.mult)
-                    if gi == 2:
-                        nc.vector.tensor_tensor(out=g_sb[:, cs], in0=g_sb[:, cs], in1=i_sb[:, cs], op=ALU.mult)
-                        nc.vector.tensor_tensor(out=c_sb[:, cs], in0=g_sb[:, cs], in1=f_sb[:, cs], op=ALU.add)
-                        nc.scalar.activation(out=tc_sb[:, cs], in_=c_sb[:, cs], func=ACT.Tanh)
+                if ADDS_FIRST:
+                    for j, (lo, n) in enumerate(cols):
+                        gate_value(gi, accs[j], lo, n)
+                    for lo, n in cols:
+                        after(gi, lo, n)
+                else:
+                    for j, (lo, n) in enumerate(cols):
+                        gate_value(gi, accs[j], lo, n)
+                        after(gi, lo, n)
             else:
+                late = []
                 for j, (lo, n) in enumerate(cols):
                     for a in range(2):
                         mx_pass(accs[j], n, GX + 1 + a, tails[j][:, a, :], 7, 1 + a, lo, False, a == 1)
                     gate_value(gi, accs[j], lo, n)
-                    if j < POOL_MULS:
+                    if ADDS_FIRST and j >= POOL_MULS:
+                        late.append(j)
+                    else:
                         h_out(j)
-                for j in range(POOL_MULS, len(cols)):
+                for j in late:
                     h_out(j)

@@ -22,7 +22,7 @@ COLS = [(0, 512), (512, 512), (1024, 512)]
 O_COLS = [(0, 512), (512, 512), (1024, 256), (1280, 256)]
 S_MODE = "mixed"
 PIN = False
-CT_LATE = False
+CT_LATE = True
 ADDS_FIRST = False
 POOL_MULS = 0
 BIAS_ON_POOL = True

@@ -64,11 +64,11 @@ def tile_lstmcell_w_kernel(
         warm2 = keep.tile([P, 8], F32, name="warm2")
         nc.scalar.activation(out=warm2[:], in_=warm[:], func=ACT.Sigmoid)
 
-        x_sb = keep.tile([P, D], BF16, name="x_sb")
+        x_sb = keep.tile([P, D], BF16, name="x_sb", align_bytes=256)
         nc.sync.dma_start(out=x_sb[:], in_=x)
-        h_sb = keep.tile([P, H], BF16, name="h_sb")
+        h_sb = keep.tile([P, H], BF16, name="h_sb", align_bytes=256)
         nc.sync.dma_start(out=h_sb[:], in_=h0)
-        c0_sb = keep.tile([P, H], BF16, name="c0_sb")
+        c0_sb = keep.tile([P, H], BF16, name="c0_sb", align_bytes=256)
 
         def scale_dma(on_sync, w, scales, groups, q):
             if on_sync:
@@ -98,7 +98,7 @@ def tile_lstmcell_w_kernel(
             eng.dma_start(out=zb[row:row + 1, bg * H:(bg + 1) * H], in_=vec.rearrange("(o n) -> o n", o=1))
 
         def load_words(words, g):
-            wt = wring.tile([P, H], U32, name="wt", tag="wt", align_bytes=64)
+            wt = wring.tile([P, H], U32, name="wt", tag="wt", align_bytes=256)
             nc.sync.dma_start(
                 out=wt[:].bitcast(I32),
                 in_=words[g].rearrange("p n t -> p (n t)").bitcast(I32),
@@ -135,7 +135,7 @@ def tile_lstmcell_w_kernel(
 
         def issue_tails():
             for j, (lo, n) in enumerate(O_COLS):
-                tl = keep.tile([P, 2, n], U32, name="tail%d" % j, align_bytes=64)
+                tl = keep.tile([P, 2, n], U32, name="tail%d" % j, align_bytes=256)
                 nc.sync.dma_start(
                     out=tl[:].bitcast(I32),
                     in_=W_ho_words[1:3, :, lo:lo + n, :].rearrange("g p n t -> p g (n t)").bitcast(I32),
@@ -180,9 +180,9 @@ def tile_lstmcell_w_kernel(
         i_sb = keep.tile([P, H], F32, name="i_sb")
         f_sb = keep.tile([P, H], F32, name="f_sb")
         g_sb = keep.tile([P, H], F32, name="g_sb")
-        c_sb = keep.tile([P, H], F32, name="c_sb")
+        c_sb = keep.tile([P, H], F32, name="c_sb", align_bytes=256)
         tc_sb = keep.tile([P, H], F32, name="tc_sb")
-        o_sb = keep.tile([P, H], F32, name="o_sb")
+        o_sb = keep.tile([P, H], F32, name="o_sb", align_bytes=256)
         dst = [i_sb, f_sb, g_sb, o_sb]
 
         def mx_pass(acc, n, xg, rhs, w, g, lo, start, stop):

@@ -50,11 +50,11 @@ def tile_lstmcell_w_kernel(
         if PIN:
             ctx.enter_context(tc.manual_schedule())
 
-        planes = keep.tile([P, 8, H], U8, name="planes", align_bytes=64)
+        planes = keep.tile([P, 8, H], U8, name="planes", align_bytes=256)
         nc.vector.memset(planes[:, 0:2, :].rearrange("p w n -> p (w n)").bitcast(I32), 0)
         warm = keep.tile([P, 8], F32, name="warm")
         nc.vector.memset(warm[:], 0.0)
-        zb = keep.tile([P, 4 * H], BF16, name="zb")
+        zb = keep.tile([P, 4 * H], BF16, name="zb", align_bytes=256)
         nc.vector.memset(zb[:].bitcast(I32), 0)
         nc.vector.memset(planes[:, 2:8, :].rearrange("p w n -> p (w n)").bitcast(I32), 0)
         ones = keep.tile([P, P], BF16, name="ones")

from contextlib import ExitStack

import concourse.mybir as mybir
from concourse.masks import make_identity

F32 = mybir.dt.float32
BF16 = mybir.dt.bfloat16
I32 = mybir.dt.int32
U32 = mybir.dt.uint32
U8 = mybir.dt.uint8
FP8X4 = mybir.dt.float8_e4m3fn_x4
ACT = mybir.ActivationFunctionType
ALU = mybir.AluOpType

P = 128
B, D, H = 128, 2048, 1536
GX = D // 512
GH = H // 512
FLOPS = 2 * B * (D + H) * 4 * H
RING = 16
COLS = [(0, 512), (512, 512), (1024, 512)]
O_COLS = [(0, 512), (512, 512), (1024, 256), (1280, 256)]
S_MODE = "mixed"
PIN = False
CT_LATE = True
ADDS_FIRST = False
POOL_MULS = 0
BIAS_ON_POOL = True


def tile_lstmcell_w_kernel(
    tc, x, h0, c0,
    W_ii_words, W_ii_scales, b_ii, W_hi_words, W_hi_scales, b_hi,
    W_if_words, W_if_scales, b_if, W_hf_words, W_hf_scales, b_hf,
    W_ig_words, W_ig_scales, b_ig, W_hg_words, W_hg_scales, b_hg,
    W_io_words, W_io_scales, b_io, W_ho_words, W_ho_scales, b_ho,
    out_0, out_1,
):
    nc = tc.nc
    gates = [
        (W_ii_words, W_ii_scales, b_ii, W_hi_words, W_hi_scales, b_hi, ACT.Sigmoid),
        (W_if_words, W_if_scales, b_if, W_hf_words, W_hf_scales, b_hf, ACT.Sigmoid),
        (W_ig_words, W_ig_scales, b_ig, W_hg_words, W_hg_scales, b_hg, ACT.Tanh),
        (W_io_words, W_io_scales, b_io, W_ho_words, W_ho_scales, b_ho, ACT.Sigmoid),
    ]
    with ExitStack() as ctx:
        keep = ctx.enter_context(tc.tile_pool(name="keep", bufs=1))
        wring = ctx.enter_context(tc.tile_pool(name="wring", bufs=RING))
        psum = ctx.enter_context(tc.psum_pool(name="psum", bufs=8))
        if PIN:
            ctx.enter_context(tc.manual_schedule())

        planes = keep.tile([P, 8, H], U8, name="planes", align_bytes=256)
        nc.vector.memset(planes[:, 0:2, :].rearrange("p w n -> p (w n)").bitcast(I32), 0)
        warm = keep.tile([P, 8], F32, name="warm")
        nc.vector.memset(warm[:], 0.0)
        zb = keep.tile([P, 4 * H], BF16, name="zb", align_bytes=256)
        nc.vector.memset(zb[:].bitcast(I32), 0)
        nc.vector.memset(planes[:, 2:8, :].rearrange("p w n -> p (w n)").bitcast(I32), 0)
        ones = keep.tile([P, P], BF16, name="ones")
        nc.vector.memset(ones[:], 1.0)
        ident = keep.tile([P, P], F32, name="ident")
        make_identity(nc, ident[:])
        warm2 = keep.tile([P, 8], F32, name="warm2")
        nc.scalar.activation(out=warm2[:], in_=warm[:], func=ACT.Sigmoid)

        x_sb = keep.tile([P, D], BF16, name="x_sb", align_bytes=256)
        nc.sync.dma_start(out=x_sb[:], in_=x)
        h_sb = keep.tile([P, H], BF16, name="h_sb", align_bytes=256)
        nc.sync.dma_start(out=h_sb[:], in_=h0)
        c0_sb = keep.tile([P, H], BF16, name="c0_sb", align_bytes=256)

        def scale_dma(on_sync, w, scales, groups, q):
            if on_sync:
                nc.sync.dma_start(
                    out=planes[32 * q:32 * q + 4 * groups, w, :].bitcast(I32),
                    in_=scales[:, 4 * q:4 * q + 4, :].bitcast(I32),
                )
            else:
                nc.gpsimd.dma_start(
                    out=planes[32 * q:32 * q + 4 * groups, w, :].bitcast(F32),
                    in_=scales[:, 4 * q:4 * q + 4, :].bitcast(F32),
                )

        woven = []
        for gi in range(4):
            for w, scales, groups in ((2 * gi, gates[gi][1], GX), (2 * gi + 1, gates[gi][4], GH)):
                for q in range(4):
                    if S_MODE == "sync" or (S_MODE == "mixed" and q < 2):
                        woven.append((w, scales, groups, q))
        biases = []
        for gi in range(4):
            biases.append((0, gi, gates[gi][2]))
            biases.append((1, gi, gates[gi][5]))
        nloads = [0]

        def bias_dma(eng, row, bg, vec):
            eng.dma_start(out=zb[row:row + 1, bg * H:(bg + 1) * H], in_=vec.rearrange("(o n) -> o n", o=1))

        def load_words(words, g):
            wt = wring.tile([P, H], U32, name="wt", tag="wt", align_bytes=256)
            nc.sync.dma_start(
                out=wt[:].bitcast(I32),
                in_=words[g].rearrange("p n t -> p (n t)").bitcast(I32),
            )
            nloads[0] = nloads[0] + 1
            count = 2 if (S_MODE == "sync" or nloads[0] <= 2) else 1
            for rep in range(count):
                if len(woven) > 0:
                    w, scales, groups, q = woven.pop(0)
                    scale_dma(True, w, scales, groups, q)
            if len(biases) > 0 and not BIAS_ON_POOL:
                row, bg, vec = biases.pop(0)
                bias_dma(nc.sync, row, bg, vec)
            return wt

        def issue_gate(gi):
            wi, si, bi, wh, sh, bh, func = gates[gi]
            for w, scales, groups in ((2 * gi, si, GX), (2 * gi + 1, sh, GH)):
                for q in range(4):
                    if S_MODE == "pool" or (S_MODE == "mixed" and q >= 2):
                        scale_dma(False, w, scales, groups, q)
            if BIAS_ON_POOL:
                bias_dma(nc.gpsimd, 0, gi, bi)
                bias_dma(nc.gpsimd, 1, gi, bh)
            full = []
            for g in range(GX):
                full.append((load_words(wi, g), 2 * gi, g, g))
            last_full = GH if gi < 3 else 1
            for g in range(last_full):
                full.append((load_words(wh, g), 2 * gi + 1, g, GX + g))
            return full

        tails = []

        def issue_tails():
            for j, (lo, n) in enumerate(O_COLS):
                tl = keep.tile([P, 2, n], U32, name="tail%d" % j, align_bytes=256)
                nc.sync.dma_start(
                    out=tl[:].bitcast(I32),
                    in_=W_ho_words[1:3, :, lo:lo + n, :].rearrange("g p n t -> p g (n t)").bitcast(I32),
                )
                tails.append(tl)

        loaded = {0: issue_gate(0)}

        grouped = keep.tile([P, 4 * (GX + GH) * P], BF16, name="grouped", align_bytes=64)
        xcodes = keep.tile([P, (GX + GH) * P], U32, name="xcodes", align_bytes=64)
        xsc = keep.tile([P, (GX + GH) * P], U8, name="xsc", align_bytes=64)
        xw = x_sb[:].bitcast(F32)
        hw = h_sb[:].bitcast(F32)
        srcs = [(xw, g) for g in range(GX)] + [(hw, g) for g in range(GH)]
        for j in range(4):
            pair = srcs[2 * j:2 * j + 2]
            s = len(pair)
            bank = psum.tile([P, 512], F32, name="tb", tag="bank")
            for a, (src, g) in enumerate(pair):
                for u in range(2):
                    nc.tensor.transpose(
                        out=bank[:, (2 * a + u) * P:(2 * a + u + 1) * P],
                        in_=src[:, 256 * g + u:256 * (g + 1):2],
                        identity=ident[:],
                    )
            rd = bank[:, 0:256 * s].rearrange("p (s u b) -> p s b u", s=s, u=2)
            wr = grouped[:, 1024 * j:1024 * j + 512 * s].bitcast(F32).rearrange(
                "p (s b u) -> p s b u", s=s, u=2)
            if j % 2 == 0:
                nc.vector.tensor_copy(out=wr, in_=rd)
            else:
                nc.scalar.copy(out=wr, in_=rd)
        for j in range(4):
            s = len(srcs[2 * j:2 * j + 2])
            nc.vector.quantize_mx(
                out=xcodes[:, 256 * j:256 * j + 128 * s].bitcast(FP8X4),
                scales=xsc[:, 256 * j:256 * j + 128 * s],
                in_=grouped[:, 1024 * j:1024 * j + 512 * s],
            )

        bias_sb = keep.tile([P, 4 * H], F32, name="bias_sb")
        i_sb = keep.tile([P, H], F32, name="i_sb")
        f_sb = keep.tile([P, H], F32, name="f_sb")
        g_sb = keep.tile([P, H], F32, name="g_sb")
        c_sb = keep.tile([P, H], F32, name="c_sb", align_bytes=256)
        tc_sb = keep.tile([P, H], F32, name="tc_sb")
        o_sb = keep.tile([P, H], F32, name="o_sb", align_bytes=256)
        dst = [i_sb, f_sb, g_sb, o_sb]

        def mx_pass(acc, n, xg, rhs, w, g, lo, start, stop):
            nc.tensor.matmul_mx(
                out=acc[:, 0:n],
                lhsT=xcodes[:, P * xg:P * (xg + 1)].bitcast(FP8X4),
                lhsT_scale=xsc[:, P * xg:P * (xg + 1)],
                rhs=rhs.bitcast(FP8X4),
                rhs_scale=planes[4 * g:P, w, lo:lo + n],
                start=start,
                stop=stop,
            )

        def spread_bias(gi):
            for c in range(3):
                lo = gi * H + 512 * c
                bb = psum.tile([P, 512], F32, name="bb", tag="bank")
                nc.tensor.matmul(out=bb[:], lhsT=ones[:], rhs=zb[:, lo:lo + 512], start=True, stop=True)
                nc.scalar.copy(out=bias_sb[:, lo:lo + 512], in_=bb[:])

        def gate_value(gi, acc, lo, n):
            t = dst[gi]
            nc.vector.tensor_tensor(out=t[:, lo:lo + n], in0=acc[:, 0:n],
                                    in1=bias_sb[:, gi * H + lo:gi * H + lo + n], op=ALU.add)
            nc.scalar.activation(out=t[:, lo:lo + n], in_=t[:, lo:lo + n], func=gates[gi][6])

        def after(gi, lo, n):
            cs = slice(lo, lo + n)
            if gi == 1:
                nc.vector.tensor_tensor(out=f_sb[:, cs], in0=f_sb[:, cs], in1=c0_sb[:, cs], op=ALU.mult)
            if gi == 2:
                nc.vector.tensor_tensor(out=g_sb[:, cs], in0=g_sb[:, cs], in1=i_sb[:, cs], op=ALU.mult)
                nc.vector.tensor_tensor(out=c_sb[:, cs], in0=g_sb[:, cs], in1=f_sb[:, cs], op=ALU.add)
                nc.scalar.activation(out=tc_sb[:, cs], in_=c_sb[:, cs], func=ACT.Tanh)
                if not CT_LATE:
                    nc.scalar.dma_start(out=out_1[:, cs], in_=c_sb[:, cs])

        def h_out(j):
            lo, n = O_COLS[j]
            cs = slice(lo, lo + n)
            eng = nc.gpsimd if j < POOL_MULS else nc.vector
            eng.tensor_tensor(out=o_sb[:, cs], in0=o_sb[:, cs], in1=tc_sb[:, cs], op=ALU.mult)
            nc.sync.dma_start(out=out_0[:, cs], in_=o_sb[:, cs])

        for gi in range(4):
            if gi == 0:
                nc.sync.dma_start(out=c0_sb[:], in_=c0)
            if gi + 1 < 4:
                loaded[gi + 1] = issue_gate(gi + 1)
                if gi + 1 == 3 and not CT_LATE:
                    issue_tails()
            if gi == 3 and CT_LATE:
                issue_tails()
                for lo, n in COLS:
                    nc.sync.dma_start(out=out_1[:, lo:lo + n], in_=c_sb[:, lo:lo + n])
            full = loaded[gi]
            cols = O_COLS if gi == 3 else COLS
            accs = []
            for j in range(len(cols)):
                acc = psum.tile([P, 512], F32, name="acc", tag="bank")
                accs.append(acc)
            npass = GX + GH
            for ki, (wt, w, g, xg) in enumerate(full):
                for j, (lo, n) in enumerate(cols):
                    mx_pass(accs[j], n, xg, wt[:, lo:lo + n], w, g, lo, ki == 0, ki == npass - 1)
                if ki == 3:
                    spread_bias(gi)
            if gi < 3:
                if ADDS_FIRST:
                    for j, (lo, n) in enumerate(cols):
                        gate_value(gi, accs[j], lo, n)
                    for lo, n in cols:
                        after(gi, lo, n)
                else:
                    for j, (lo, n) in enumerate(cols):
                        gate_value(gi, accs[j], lo, n)
                        after(gi, lo, n)
            else:
                late = []
                for j, (lo, n) in enumerate(cols):
                    for a in range(2):
                        mx_pass(accs[j], n, GX + 1 + a, tails[j][:, a, :], 7, 1 + a, lo, False, a == 1)
                    gate_value(gi, accs[j], lo, n)
                    if ADDS_FIRST and j >= POOL_MULS:
                        late.append(j)
                    else:
                        h_out(j)
                for j in late:
                    h_out(j)
